import numpy as np
import ml_dtypes

BF16 = ml_dtypes.bfloat16


def bf(x):
    return np.asarray(x, np.float32).astype(BF16)


def f32(x):
    return np.asarray(x, np.float32)


def f64(x):
    return np.asarray(x).astype(np.float64)


def striped(idx):
    return np.tile(idx.reshape(-1, 16).T, (8, 1))


B, D, C, S, N = 4, 128, 512, 1024, 256


def setup_inputs():
    q = bf(2.0 * np.random.standard_normal((C, N)))
    k = bf(np.random.standard_normal((C, S)))
    v = f32(np.random.standard_normal((C, S)) + 0.5 * np.random.standard_normal((C, 1)))
    return {"q": q, "k": k, "v": v, "offs": striped(np.random.permutation(S)[:N])}


def reference(q, k, v, offs):
    idx = offs[:16].T.reshape(-1)
    out = np.zeros((C, S))
    for i in range(B):
        r = slice(i * D, (i + 1) * D)
        e = np.exp(f64(k)[r].T @ f64(q)[r] / np.sqrt(D))
        num = f64(v)[r] @ e
        ctx = num * (1.0 / e.sum(axis=0, keepdims=True))
        blk = np.repeat(ctx.mean(axis=1, keepdims=True), S, axis=1)
        blk[:, idx] = ctx
        out[r] = blk
    return out

@@ -1,0 +1,92 @@
+import math
+
+import concourse.mybir as mybir
+from concourse.masks import make_identity
+
+SEQS = 4
+D = 128
+S = 1024
+N = 256
+KEY_BLOCKS = S // 128
+
+F32 = mybir.dt.float32
+BF16 = mybir.dt.bfloat16
+U16 = mybir.dt.uint16
+MULT = mybir.AluOpType.mult
+EXP = mybir.ActivationFunctionType.Exp
+
+FLOPS = 2 * (2 * SEQS * D * S * N)
+
+
+def tile_informermodel_s_kernel(tc, q, k, v, offs, out):
+    nc = tc.nc
+    with (
+        tc.tile_pool(name="held", bufs=1) as held,
+        tc.tile_pool(name="inputs", bufs=SEQS) as inputs,
+        tc.tile_pool(name="work", bufs=2) as work,
+        tc.psum_pool(name="flipped", bufs=2) as flipped,
+        tc.psum_pool(name="scores", bufs=2) as scores,
+        tc.psum_pool(name="sums", bufs=2) as sums,
+    ):
+        offsets = held.tile([128, N // 16], U16, name="offsets")
+        nc.sync.dma_start(offsets[:], offs)
+
+        q_tiles, k_tiles, v_tiles = [], [], []
+        for i in range(SEQS):
+            rows = slice(i * D, (i + 1) * D)
+            q_i = inputs.tile([D, N], BF16, name="q_i")
+            k_i = inputs.tile([D, S], BF16, name="k_i")
+            v_i = inputs.tile([D, S], F32, name="v_i")
+            nc.sync.dma_start(q_i[:], q[rows, :])
+            nc.sync.dma_start(k_i[:], k[rows, :])
+            nc.sync.dma_start(v_i[:], v[rows, :])
+            q_tiles.append(q_i)
+            k_tiles.append(k_i)
+            v_tiles.append(v_i)
+
+        identity = held.tile([128, 128], F32, name="identity")
+        make_identity(nc, identity[:])
+        ones = held.tile([128, D], BF16, name="ones")
+        nc.vector.memset(ones[:], 1.0)
+
+        for i in range(SEQS):
+            q_i, k_i, v_i = q_tiles[i], k_tiles[i], v_tiles[i]
+
+            v_flipped = work.tile([128, KEY_BLOCKS, D], BF16, name="v_flipped")
+            for first in range(0, KEY_BLOCKS, 4):
+                bank = flipped.tile([128, 4, D], F32, name="bank")
+                for b in range(4):
+                    keys = slice((first + b) * 128, (first + b + 1) * 128)
+                    nc.tensor.transpose(bank[:, b, :], v_i[:, keys], identity[:])
+                nc.vector.tensor_copy(v_flipped[:, first : first + 4, :], bank[:])
+
+            e = work.tile([128, KEY_BLOCKS, N], BF16, name="e")
+            for first in range(0, KEY_BLOCKS, 2):
+                score = scores.tile([128, 2, N], F32, name="score")
+                for b in range(2):
+                    keys = slice((first + b) * 128, (first + b + 1) * 128)
+                    nc.tensor.matmul(score[:, b, :], k_i[:, keys], q_i[:], start=True, stop=True)
+                nc.scalar.activation(e[:, first : first + 2, :], score[:], EXP, scale=1.0 / math.sqrt(D))
+
+            num_sum = sums.tile([D, N], F32, name="num_sum")
+            den = sums.tile([D, N], F32, name="den")
+            for b in range(KEY_BLOCKS):
+                nc.tensor.matmul(num_sum[:], v_flipped[:, b, :], e[:, b, :], start=(b == 0), stop=(b == KEY_BLOCKS - 1))
+            for b in range(KEY_BLOCKS):
+                nc.tensor.matmul(den[:], ones[:], e[:, b, :], start=(b == 0), stop=(b == KEY_BLOCKS - 1))
+
+            num = work.tile([D, N], F32, name="num")
+            nc.scalar.copy(num[:], num_sum[:])
+            over_den = work.tile([D, N], F32, name="over_den")
+            nc.vector.reciprocal(over_den[:], den[:])
+
+            ctx = work.tile([D, N], F32, name="ctx")
+            nc.vector.tensor_tensor(ctx[:], num[:], over_den[:], MULT)
+            total = work.tile([D, 1], F32, name="total")
+            nc.vector.reduce_sum(total[:], ctx[:], axis=mybir.AxisListType.X)
+
+            window = work.tile([D, S], F32, name="window")
+            nc.vector.tensor_scalar(window[:], total[:].to_broadcast([D, S]), 1.0 / N, None, MULT)
+
+            nc.vector.tensor_tensor(window[:].indirect(offsets[:]), num[:], over_den[:], MULT)
+            nc.sync.dma_start(out[i * D : (i + 1) * D, :], window[:])

@@ -8,6 +8,7 @@ D = 128
 S = 1024
 N = 256
 KEY_BLOCKS = S // 128
+QUERY_BLOCKS = N // 128
 
 F32 = mybir.dt.float32
 BF16 = mybir.dt.bfloat16
@@ -27,6 +28,7 @@ def tile_informermodel_s_kernel(tc, q, k, v, offs, out):
         tc.psum_pool(name="flipped", bufs=2) as flipped,
         tc.psum_pool(name="scores", bufs=2) as scores,
         tc.psum_pool(name="sums", bufs=2) as sums,
+        tc.psum_pool(name="norms", bufs=1) as norms,
     ):
         offsets = held.tile([128, N // 16], U16, name="offsets")
         nc.sync.dma_start(offsets[:], offs)
@@ -46,7 +48,7 @@ def tile_informermodel_s_kernel(tc, q, k, v, offs, out):
 
         identity = held.tile([128, 128], F32, name="identity")
         make_identity(nc, identity[:])
-        ones = held.tile([128, D], BF16, name="ones")
+        ones = held.tile([128, 1], BF16, name="ones")
         nc.vector.memset(ones[:], 1.0)
 
         for i in range(SEQS):
@@ -69,16 +71,29 @@ def tile_informermodel_s_kernel(tc, q, k, v, offs, out):
                 nc.scalar.activation(e[:, first : first + 2, :], score[:], EXP, scale=1.0 / math.sqrt(D))
 
             num_sum = sums.tile([D, N], F32, name="num_sum")
-            den = sums.tile([D, N], F32, name="den")
             for b in range(KEY_BLOCKS):
                 nc.tensor.matmul(num_sum[:], v_flipped[:, b, :], e[:, b, :], start=(b == 0), stop=(b == KEY_BLOCKS - 1))
-            for b in range(KEY_BLOCKS):
-                nc.tensor.matmul(den[:], ones[:], e[:, b, :], start=(b == 0), stop=(b == KEY_BLOCKS - 1))
+
+            den = norms.tile([128, QUERY_BLOCKS], F32, name="den")
+            for jb in range(QUERY_BLOCKS):
+                queries = slice(jb * 128, (jb + 1) * 128)
+                for b in range(KEY_BLOCKS):
+                    nc.tensor.matmul(
+                        den[:, jb : jb + 1], e[:, b, queries], ones[:], start=(b == 0), stop=(b == KEY_BLOCKS - 1)
+                    )
+            over_den_column = work.tile([128, QUERY_BLOCKS], F32, name="over_den_column")
+            nc.vector.reciprocal(over_den_column[:], den[:])
+
+            spread = norms.tile([D, N], F32, name="spread")
+            for jb in range(QUERY_BLOCKS):
+                queries = slice(jb * 128, (jb + 1) * 128)
+                repeated = over_den_column[:, jb : jb + 1].to_broadcast([128, D])
+                nc.tensor.transpose(spread[:, queries], repeated, identity[:])
 
             num = work.tile([D, N], F32, name="num")
             nc.scalar.copy(num[:], num_sum[:])
             over_den = work.tile([D, N], F32, name="over_den")
-            nc.vector.reciprocal(over_den[:], den[:])
+            nc.vector.tensor_copy(over_den[:], spread[:])
 
             ctx = work.tile([D, N], F32, name="ctx")
             nc.vector.tensor_tensor(ctx[:], num[:], over_den[:], MULT)

@@ -19,89 +19,116 @@ EXP = mybir.ActivationFunctionType.Exp
 FLOPS = 2 * (2 * SEQS * D * S * N)
 
 
+def attend(nc, per_seq, scores, others, q_i, k_i, v_i, identity_bf16):
+    e = per_seq.tile([128, KEY_BLOCKS, N], BF16, name="e")
+    for first in range(0, KEY_BLOCKS, 2):
+        score = scores.tile([128, 2, N], F32, name="score")
+        for b in range(2):
+            keys = slice((first + b) * 128, (first + b + 1) * 128)
+            nc.tensor.matmul(score[:, b, :], k_i[:, keys], q_i[:], start=True, stop=True)
+        nc.scalar.activation(e[:, first : first + 2, :], score[:], EXP, scale=1.0 / math.sqrt(D))
+
+    v_rounded = per_seq.tile([D, S], BF16, name="v_rounded")
+    nc.gpsimd.tensor_copy(v_rounded[:], v_i[:])
+    flipped = others.tile([128, KEY_BLOCKS, D], BF16, name="flipped")
+    for b in range(KEY_BLOCKS):
+        keys = slice(b * 128, (b + 1) * 128)
+        nc.tensor.transpose(flipped[:, b, :], v_rounded[:, keys], identity_bf16[:])
+    v_flipped = per_seq.tile([128, KEY_BLOCKS, D], BF16, name="v_flipped")
+    nc.vector.tensor_copy(v_flipped[:], flipped[:])
+    return e, v_flipped
+
+
+def reciprocal_of_den(nc, per_seq, others, e, ones):
+    den = others.tile([128, QUERY_BLOCKS], F32, name="den")
+    for jb in range(QUERY_BLOCKS):
+        queries = slice(jb * 128, (jb + 1) * 128)
+        for b in range(KEY_BLOCKS):
+            nc.tensor.matmul(den[:, jb : jb + 1], e[:, b, queries], ones[:], start=(b == 0), stop=(b == KEY_BLOCKS - 1))
+    over_den_column = per_seq.tile([128, QUERY_BLOCKS], F32, name="over_den_column")
+    nc.vector.reciprocal(over_den_column[:], den[:])
+    return over_den_column
+
+
+def sum_num(nc, per_seq, others, e, v_flipped):
+    num_sum = others.tile([D, N], F32, name="num_sum")
+    for b in range(KEY_BLOCKS):
+        nc.tensor.matmul(num_sum[:], v_flipped[:, b, :], e[:, b, :], start=(b == 0), stop=(b == KEY_BLOCKS - 1))
+    num = per_seq.tile([D, N], F32, name="num")
+    nc.scalar.copy(num[:], num_sum[:])
+    return num
+
+
+def spread_over_partitions(nc, per_seq, others, over_den_column, identity):
+    spread = others.tile([D, N], F32, name="spread")
+    for jb in range(QUERY_BLOCKS):
+        queries = slice(jb * 128, (jb + 1) * 128)
+        repeated = over_den_column[:, jb : jb + 1].to_broadcast([128, D])
+        nc.tensor.transpose(spread[:, queries], repeated, identity[:])
+    over_den = per_seq.tile([D, N], F32, name="over_den")
+    nc.scalar.copy(over_den[:], spread[:])
+    return over_den
+
+
 def tile_informermodel_s_kernel(tc, q, k, v, offs, out):
     nc = tc.nc
     with (
         tc.tile_pool(name="held", bufs=1) as held,
-        tc.tile_pool(name="inputs", bufs=SEQS) as inputs,
-        tc.tile_pool(name="work", bufs=2) as work,
-        tc.psum_pool(name="flipped", bufs=2) as flipped,
-        tc.psum_pool(name="scores", bufs=2) as scores,
-        tc.psum_pool(name="sums", bufs=2) as sums,
-        tc.psum_pool(name="norms", bufs=1) as norms,
+        tc.tile_pool(name="per_seq", bufs=SEQS) as per_seq,
+        tc.psum_pool(name="scores", bufs=4) as scores,
+        tc.psum_pool(name="others", bufs=1) as others,
     ):
-        offsets = held.tile([128, N // 16], U16, name="offsets")
-        nc.sync.dma_start(offsets[:], offs)
-
         q_tiles, k_tiles, v_tiles = [], [], []
         for i in range(SEQS):
             rows = slice(i * D, (i + 1) * D)
-            q_i = inputs.tile([D, N], BF16, name="q_i")
-            k_i = inputs.tile([D, S], BF16, name="k_i")
-            v_i = inputs.tile([D, S], F32, name="v_i")
+            q_i = per_seq.tile([D, N], BF16, name="q_i")
+            k_i = per_seq.tile([D, S], BF16, name="k_i")
+            v_i = per_seq.tile([D, S], F32, name="v_i")
             nc.sync.dma_start(q_i[:], q[rows, :])
             nc.sync.dma_start(k_i[:], k[rows, :])
             nc.sync.dma_start(v_i[:], v[rows, :])
             q_tiles.append(q_i)
             k_tiles.append(k_i)
             v_tiles.append(v_i)
+        offsets = held.tile([128, N // 16], U16, name="offsets")
+        nc.sync.dma_start(offsets[:], offs)
 
         identity = held.tile([128, 128], F32, name="identity")
         make_identity(nc, identity[:])
+        identity_bf16 = held.tile([128, 128], BF16, name="identity_bf16")
+        make_identity(nc, identity_bf16[:])
         ones = held.tile([128, 1], BF16, name="ones")
         nc.vector.memset(ones[:], 1.0)
 
-        for i in range(SEQS):
-            q_i, k_i, v_i = q_tiles[i], k_tiles[i], v_tiles[i]
-
-            v_flipped = work.tile([128, KEY_BLOCKS, D], BF16, name="v_flipped")
-            for first in range(0, KEY_BLOCKS, 4):
-                bank = flipped.tile([128, 4, D], F32, name="bank")
-                for b in range(4):
-                    keys = slice((first + b) * 128, (first + b + 1) * 128)
-                    nc.tensor.transpose(bank[:, b, :], v_i[:, keys], identity[:])
-                nc.vector.tensor_copy(v_flipped[:, first : first + 4, :], bank[:])
-
-            e = work.tile([128, KEY_BLOCKS, N], BF16, name="e")
-            for first in range(0, KEY_BLOCKS, 2):
-                score = scores.tile([128, 2, N], F32, name="score")
-                for b in range(2):
-                    keys = slice((first + b) * 128, (first + b + 1) * 128)
-                    nc.tensor.matmul(score[:, b, :], k_i[:, keys], q_i[:], start=True, stop=True)
-                nc.scalar.activation(e[:, first : first + 2, :], score[:], EXP, scale=1.0 / math.sqrt(D))
-
-            num_sum = sums.tile([D, N], F32, name="num_sum")
-            for b in range(KEY_BLOCKS):
-                nc.tensor.matmul(num_sum[:], v_flipped[:, b, :], e[:, b, :], start=(b == 0), stop=(b == KEY_BLOCKS - 1))
-
-            den = norms.tile([128, QUERY_BLOCKS], F32, name="den")
-            for jb in range(QUERY_BLOCKS):
-                queries = slice(jb * 128, (jb + 1) * 128)
-                for b in range(KEY_BLOCKS):
-                    nc.tensor.matmul(
-                        den[:, jb : jb + 1], e[:, b, queries], ones[:], start=(b == 0), stop=(b == KEY_BLOCKS - 1)
+        attended = [
+            attend(nc, per_seq, scores, others, q_tiles[i], k_tiles[i], v_tiles[i], identity_bf16) for i in range(2)
+        ]
+        windows, nums, over_dens = [], [], []
+        for i in range(SEQS + 1):
+            if i < SEQS:
+                e, v_flipped = attended[i]
+                over_den_column = reciprocal_of_den(nc, per_seq, others, e, ones)
+            if i > 0:
+                nc.vector.tensor_tensor(
+                    windows[i - 1][:].indirect(offsets[:]), nums[i - 1][:], over_dens[i - 1][:], MULT
+                )
+                nc.sync.dma_start(out[(i - 1) * D : i * D, :], windows[i - 1][:])
+            if i < SEQS:
+                num = sum_num(nc, per_seq, others, e, v_flipped)
+                over_den = spread_over_partitions(nc, per_seq, others, over_den_column, identity)
+                scaled_ctx = per_seq.tile([D, N], F32, name="scaled_ctx")
+                mean = per_seq.tile([D, 1], F32, name="mean")
+                nc.vector.scalar_tensor_tensor(
+                    scaled_ctx[:], num[:], 1.0 / N, over_den[:], MULT, MULT, accum_out=mean[:]
+                )
+                if i + 2 < SEQS:
+                    attended.append(
+                        attend(
+                            nc, per_seq, scores, others, q_tiles[i + 2], k_tiles[i + 2], v_tiles[i + 2], identity_bf16
+                        )
                     )
-            over_den_column = work.tile([128, QUERY_BLOCKS], F32, name="over_den_column")
-            nc.vector.reciprocal(over_den_column[:], den[:])
-
-            spread = norms.tile([D, N], F32, name="spread")
-            for jb in range(QUERY_BLOCKS):
-                queries = slice(jb * 128, (jb + 1) * 128)
-                repeated = over_den_column[:, jb : jb + 1].to_broadcast([128, D])
-                nc.tensor.transpose(spread[:, queries], repeated, identity[:])
-
-            num = work.tile([D, N], F32, name="num")
-            nc.scalar.copy(num[:], num_sum[:])
-            over_den = work.tile([D, N], F32, name="over_den")
-            nc.vector.tensor_copy(over_den[:], spread[:])
-
-            ctx = work.tile([D, N], F32, name="ctx")
-            nc.vector.tensor_tensor(ctx[:], num[:], over_den[:], MULT)
-            total = work.tile([D, 1], F32, name="total")
-            nc.vector.reduce_sum(total[:], ctx[:], axis=mybir.AxisListType.X)
-
-            window = work.tile([D, S], F32, name="window")
-            nc.vector.tensor_scalar(window[:], total[:].to_broadcast([D, S]), 1.0 / N, None, MULT)
-
-            nc.vector.tensor_tensor(window[:].indirect(offsets[:]), num[:], over_den[:], MULT)
-            nc.sync.dma_start(out[i * D : (i + 1) * D, :], window[:])
+                window = per_seq.tile([D, S], F32, name="window")
+                nc.vector.tensor_copy(window[:], mean[:].to_broadcast([D, S]))
+                windows.append(window)
+                nums.append(num)
+                over_dens.append(over_den)

@@ -19,7 +19,7 @@ EXP = mybir.ActivationFunctionType.Exp
 FLOPS = 2 * (2 * SEQS * D * S * N)
 
 
-def attend(nc, per_seq, scores, others, q_i, k_i, v_i, identity_bf16):
+def exp_of_scores(nc, per_seq, scores, q_i, k_i):
     e = per_seq.tile([128, KEY_BLOCKS, N], BF16, name="e")
     for first in range(0, KEY_BLOCKS, 2):
         score = scores.tile([128, 2, N], F32, name="score")
@@ -27,16 +27,17 @@ def attend(nc, per_seq, scores, others, q_i, k_i, v_i, identity_bf16):
             keys = slice((first + b) * 128, (first + b + 1) * 128)
             nc.tensor.matmul(score[:, b, :], k_i[:, keys], q_i[:], start=True, stop=True)
         nc.scalar.activation(e[:, first : first + 2, :], score[:], EXP, scale=1.0 / math.sqrt(D))
+    return e
 
-    v_rounded = per_seq.tile([D, S], BF16, name="v_rounded")
-    nc.gpsimd.tensor_copy(v_rounded[:], v_i[:])
+
+def flip(nc, per_seq, others, v_rounded, identity_bf16):
     flipped = others.tile([128, KEY_BLOCKS, D], BF16, name="flipped")
     for b in range(KEY_BLOCKS):
         keys = slice(b * 128, (b + 1) * 128)
         nc.tensor.transpose(flipped[:, b, :], v_rounded[:, keys], identity_bf16[:])
     v_flipped = per_seq.tile([128, KEY_BLOCKS, D], BF16, name="v_flipped")
     nc.vector.tensor_copy(v_flipped[:], flipped[:])
-    return e, v_flipped
+    return v_flipped
 
 
 def reciprocal_of_den(nc, per_seq, others, e, ones):
@@ -50,15 +51,6 @@ def reciprocal_of_den(nc, per_seq, others, e, ones):
     return over_den_column
 
 
-def sum_num(nc, per_seq, others, e, v_flipped):
-    num_sum = others.tile([D, N], F32, name="num_sum")
-    for b in range(KEY_BLOCKS):
-        nc.tensor.matmul(num_sum[:], v_flipped[:, b, :], e[:, b, :], start=(b == 0), stop=(b == KEY_BLOCKS - 1))
-    num = per_seq.tile([D, N], F32, name="num")
-    nc.scalar.copy(num[:], num_sum[:])
-    return num
-
-
 def spread_over_partitions(nc, per_seq, others, over_den_column, identity):
     spread = others.tile([D, N], F32, name="spread")
     for jb in range(QUERY_BLOCKS):
@@ -68,6 +60,11 @@ def spread_over_partitions(nc, per_seq, others, over_den_column, identity):
     over_den = per_seq.tile([D, N], F32, name="over_den")
     nc.scalar.copy(over_den[:], spread[:])
     return over_den
+
+
+def place_and_store(nc, window, num, over_den, offsets, out_rows):
+    nc.vector.tensor_tensor(window[:].indirect(offsets[:]), num[:], over_den[:], MULT)
+    nc.sync.dma_start(out_rows, window[:])
 
 
 def tile_informermodel_s_kernel(tc, q, k, v, offs, out):
@@ -100,35 +97,40 @@ def tile_informermodel_s_kernel(tc, q, k, v, offs, out):
         ones = held.tile([128, 1], BF16, name="ones")
         nc.vector.memset(ones[:], 1.0)
 
-        attended = [
-            attend(nc, per_seq, scores, others, q_tiles[i], k_tiles[i], v_tiles[i], identity_bf16) for i in range(2)
-        ]
-        windows, nums, over_dens = [], [], []
-        for i in range(SEQS + 1):
-            if i < SEQS:
-                e, v_flipped = attended[i]
-                over_den_column = reciprocal_of_den(nc, per_seq, others, e, ones)
-            if i > 0:
-                nc.vector.tensor_tensor(
-                    windows[i - 1][:].indirect(offsets[:]), nums[i - 1][:], over_dens[i - 1][:], MULT
-                )
-                nc.sync.dma_start(out[(i - 1) * D : i * D, :], windows[i - 1][:])
-            if i < SEQS:
-                num = sum_num(nc, per_seq, others, e, v_flipped)
-                over_den = spread_over_partitions(nc, per_seq, others, over_den_column, identity)
-                scaled_ctx = per_seq.tile([D, N], F32, name="scaled_ctx")
-                mean = per_seq.tile([D, 1], F32, name="mean")
-                nc.vector.scalar_tensor_tensor(
-                    scaled_ctx[:], num[:], 1.0 / N, over_den[:], MULT, MULT, accum_out=mean[:]
-                )
-                if i + 2 < SEQS:
-                    attended.append(
-                        attend(
-                            nc, per_seq, scores, others, q_tiles[i + 2], k_tiles[i + 2], v_tiles[i + 2], identity_bf16
-                        )
-                    )
-                window = per_seq.tile([D, S], F32, name="window")
-                nc.vector.tensor_copy(window[:], mean[:].to_broadcast([D, S]))
-                windows.append(window)
-                nums.append(num)
-                over_dens.append(over_den)
+        v_rounded_tiles = []
+        for i in range(SEQS):
+            v_rounded = per_seq.tile([D, S], BF16, name="v_rounded")
+            nc.gpsimd.tensor_copy(v_rounded[:], v_tiles[i][:])
+            v_rounded_tiles.append(v_rounded)
+
+        e_tiles = [exp_of_scores(nc, per_seq, scores, q_tiles[0], k_tiles[0])]
+        v_flipped = flip(nc, per_seq, others, v_rounded_tiles[0], identity_bf16)
+        e_tiles.append(exp_of_scores(nc, per_seq, scores, q_tiles[1], k_tiles[1]))
+        to_place = None
+        for i in range(SEQS):
+            e = e_tiles[i]
+            over_den_column = reciprocal_of_den(nc, per_seq, others, e, ones)
+            if to_place is not None:
+                place_and_store(nc, *to_place)
+
+            num_sum = others.tile([D, N], F32, name="num_sum")
+            for b in range(KEY_BLOCKS):
+                nc.tensor.matmul(num_sum[:], v_flipped[:, b, :], e[:, b, :], start=(b == 0), stop=(b == KEY_BLOCKS - 1))
+            over_den = spread_over_partitions(nc, per_seq, others, over_den_column, identity)
+
+            scaled_ctx = per_seq.tile([D, N], F32, name="scaled_ctx")
+            mean = per_seq.tile([D, 1], F32, name="mean")
+            nc.vector.scalar_tensor_tensor(
+                scaled_ctx[:], num_sum[:], 1.0 / N, over_den[:], MULT, MULT, accum_out=mean[:]
+            )
+            num = per_seq.tile([D, N], F32, name="num")
+            nc.scalar.copy(num[:], num_sum[:])
+
+            if i + 1 < SEQS:
+                v_flipped = flip(nc, per_seq, others, v_rounded_tiles[i + 1], identity_bf16)
+            window = per_seq.tile([D, S], F32, name="window")
+            nc.vector.tensor_copy(window[:], mean[:].to_broadcast([D, S]))
+            to_place = (window, num, over_den, offsets, out[i * D : (i + 1) * D, :])
+            if i + 2 < SEQS:
+                e_tiles.append(exp_of_scores(nc, per_seq, scores, q_tiles[i + 2], k_tiles[i + 2]))
+        place_and_store(nc, *to_place)

@@ -104,12 +104,14 @@ def tile_informermodel_s_kernel(tc, q, k, v, offs, out):
             v_rounded_tiles.append(v_rounded)
 
         e_tiles = [exp_of_scores(nc, per_seq, scores, q_tiles[0], k_tiles[0])]
-        v_flipped = flip(nc, per_seq, others, v_rounded_tiles[0], identity_bf16)
+        v_flipped_tiles = [flip(nc, per_seq, others, v_rounded_tiles[0], identity_bf16)]
         e_tiles.append(exp_of_scores(nc, per_seq, scores, q_tiles[1], k_tiles[1]))
         to_place = None
         for i in range(SEQS):
-            e = e_tiles[i]
+            e, v_flipped = e_tiles[i], v_flipped_tiles[i]
             over_den_column = reciprocal_of_den(nc, per_seq, others, e, ones)
+            if i + 1 < SEQS:
+                v_flipped_tiles.append(flip(nc, per_seq, others, v_rounded_tiles[i + 1], identity_bf16))
             if to_place is not None:
                 place_and_store(nc, *to_place)
 
@@ -117,20 +119,16 @@ def tile_informermodel_s_kernel(tc, q, k, v, offs, out):
             for b in range(KEY_BLOCKS):
                 nc.tensor.matmul(num_sum[:], v_flipped[:, b, :], e[:, b, :], start=(b == 0), stop=(b == KEY_BLOCKS - 1))
             over_den = spread_over_partitions(nc, per_seq, others, over_den_column, identity)
-
-            scaled_ctx = per_seq.tile([D, N], F32, name="scaled_ctx")
-            mean = per_seq.tile([D, 1], F32, name="mean")
-            nc.vector.scalar_tensor_tensor(
-                scaled_ctx[:], num_sum[:], 1.0 / N, over_den[:], MULT, MULT, accum_out=mean[:]
-            )
             num = per_seq.tile([D, N], F32, name="num")
             nc.scalar.copy(num[:], num_sum[:])
 
-            if i + 1 < SEQS:
-                v_flipped = flip(nc, per_seq, others, v_rounded_tiles[i + 1], identity_bf16)
+            scaled_ctx = per_seq.tile([D, N], F32, name="scaled_ctx")
+            mean = per_seq.tile([D, 1], F32, name="mean")
+            nc.vector.scalar_tensor_tensor(scaled_ctx[:], num[:], 1.0 / N, over_den[:], MULT, MULT, accum_out=mean[:])
+
+            if i + 2 < SEQS:
+                e_tiles.append(exp_of_scores(nc, per_seq, scores, q_tiles[i + 2], k_tiles[i + 2]))
             window = per_seq.tile([D, S], F32, name="window")
             nc.vector.tensor_copy(window[:], mean[:].to_broadcast([D, S]))
             to_place = (window, num, over_den, offsets, out[i * D : (i + 1) * D, :])
-            if i + 2 < SEQS:
-                e_tiles.append(exp_of_scores(nc, per_seq, scores, q_tiles[i + 2], k_tiles[i + 2]))
         place_and_store(nc, *to_place)

@@ -96,6 +96,8 @@ def tile_informermodel_s_kernel(tc, q, k, v, offs, out):
         make_identity(nc, identity_bf16[:])
         ones = held.tile([128, 1], BF16, name="ones")
         nc.vector.memset(ones[:], 1.0)
+        zeros = held.tile([D, S], F32, name="zeros")
+        nc.vector.memset(zeros[:], 0.0)
 
         v_rounded_tiles = []
         for i in range(SEQS):
@@ -129,6 +131,6 @@ def tile_informermodel_s_kernel(tc, q, k, v, offs, out):
             if i + 2 < SEQS:
                 e_tiles.append(exp_of_scores(nc, per_seq, scores, q_tiles[i + 2], k_tiles[i + 2]))
             window = per_seq.tile([D, S], F32, name="window")
-            nc.vector.tensor_copy(window[:], mean[:].to_broadcast([D, S]))
+            nc.vector.tensor_scalar_add(window[:], zeros[:], mean[:])
             to_place = (window, num, over_den, offsets, out[i * D : (i + 1) * D, :])
         place_and_store(nc, *to_place)

@@ -9,6 +9,11 @@ S = 1024
 N = 256
 KEY_BLOCKS = S // 128
 QUERY_BLOCKS = N // 128
+HALF = S // 2
+PAIRS = KEY_BLOCKS // 2
+STEPS = SEQS * PAIRS
+SCORE_BANKS = 4
+SCORES_AHEAD = SCORE_BANKS - 1
 
 F32 = mybir.dt.float32
 BF16 = mybir.dt.bfloat16
@@ -19,24 +24,25 @@ EXP = mybir.ActivationFunctionType.Exp
 FLOPS = 2 * (2 * SEQS * D * S * N)
 
 
-def exp_of_scores(nc, per_seq, scores, q_i, k_i):
-    e = per_seq.tile([128, KEY_BLOCKS, N], BF16, name="e")
-    for first in range(0, KEY_BLOCKS, 2):
-        score = scores.tile([128, 2, N], F32, name="score")
-        for b in range(2):
-            keys = slice((first + b) * 128, (first + b + 1) * 128)
-            nc.tensor.matmul(score[:, b, :], k_i[:, keys], q_i[:], start=True, stop=True)
-        nc.scalar.activation(e[:, first : first + 2, :], score[:], EXP, scale=1.0 / math.sqrt(D))
-    return e
+def blocks_of(pair):
+    return (2 * pair, 2 * pair + 1)
 
 
-def flip(nc, per_seq, others, v_rounded, identity_bf16):
+def make_scores(nc, scores, q_i, k_i, pair):
+    score = scores.tile([128, 2, N], F32, name="score")
+    for half, b in enumerate(blocks_of(pair)):
+        nc.tensor.matmul(score[:, half, :], k_i[:, b * 128 : (b + 1) * 128], q_i[:], start=True, stop=True)
+    return score
+
+
+def flip(nc, per_seq, others, v_rounded_halves, identity_bf16):
     flipped = others.tile([128, KEY_BLOCKS, D], BF16, name="flipped")
-    for b in range(KEY_BLOCKS):
-        keys = slice(b * 128, (b + 1) * 128)
-        nc.tensor.transpose(flipped[:, b, :], v_rounded[:, keys], identity_bf16[:])
     v_flipped = per_seq.tile([128, KEY_BLOCKS, D], BF16, name="v_flipped")
-    nc.vector.tensor_copy(v_flipped[:], flipped[:])
+    for h, v_rounded in enumerate(v_rounded_halves):
+        first = h * KEY_BLOCKS // 2
+        for b in range(KEY_BLOCKS // 2):
+            nc.tensor.transpose(flipped[:, first + b, :], v_rounded[:, b * 128 : (b + 1) * 128], identity_bf16[:])
+        nc.vector.tensor_copy(v_flipped[:, first : first + KEY_BLOCKS // 2, :], flipped[:, first : first + KEY_BLOCKS // 2, :])
     return v_flipped
 
 
@@ -51,20 +57,12 @@ def reciprocal_of_den(nc, per_seq, others, e, ones):
     return over_den_column
 
 
-def spread_over_partitions(nc, per_seq, others, over_den_column, identity):
+def spread_over_partitions(nc, others, over_den_column, identity):
     spread = others.tile([D, N], F32, name="spread")
     for jb in range(QUERY_BLOCKS):
-        queries = slice(jb * 128, (jb + 1) * 128)
         repeated = over_den_column[:, jb : jb + 1].to_broadcast([128, D])
-        nc.tensor.transpose(spread[:, queries], repeated, identity[:])
-    over_den = per_seq.tile([D, N], F32, name="over_den")
-    nc.scalar.copy(over_den[:], spread[:])
-    return over_den
-
-
-def place_and_store(nc, window, num, over_den, offsets, out_rows):
-    nc.vector.tensor_tensor(window[:].indirect(offsets[:]), num[:], over_den[:], MULT)
-    nc.sync.dma_start(out_rows, window[:])
+        nc.tensor.transpose(spread[:, jb * 128 : (jb + 1) * 128], repeated, identity[:])
+    return spread
 
 
 def tile_informermodel_s_kernel(tc, q, k, v, offs, out):
@@ -72,7 +70,8 @@ def tile_informermodel_s_kernel(tc, q, k, v, offs, out):
     with (
         tc.tile_pool(name="held", bufs=1) as held,
         tc.tile_pool(name="per_seq", bufs=SEQS) as per_seq,
-        tc.psum_pool(name="scores", bufs=4) as scores,
+        tc.tile_pool(name="per_half", bufs=2 * SEQS) as per_half,
+        tc.psum_pool(name="scores", bufs=SCORE_BANKS) as scores,
         tc.psum_pool(name="others", bufs=1) as others,
     ):
         q_tiles, k_tiles, v_tiles = [], [], []
@@ -80,13 +79,19 @@ def tile_informermodel_s_kernel(tc, q, k, v, offs, out):
             rows = slice(i * D, (i + 1) * D)
             q_i = per_seq.tile([D, N], BF16, name="q_i")
             k_i = per_seq.tile([D, S], BF16, name="k_i")
-            v_i = per_seq.tile([D, S], F32, name="v_i")
             nc.sync.dma_start(q_i[:], q[rows, :])
-            nc.sync.dma_start(k_i[:], k[rows, :])
-            nc.sync.dma_start(v_i[:], v[rows, :])
+            pieces = PAIRS if i == 0 else 1
+            for piece in range(pieces):
+                columns = slice(piece * S // pieces, (piece + 1) * S // pieces)
+                nc.sync.dma_start(k_i[:, columns], k[rows, columns])
+            v_halves = []
+            for h in range(2):
+                v_half = per_half.tile([D, HALF], F32, name="v_half")
+                nc.sync.dma_start(v_half[:], v[rows, h * HALF : (h + 1) * HALF])
+                v_halves.append(v_half)
             q_tiles.append(q_i)
             k_tiles.append(k_i)
-            v_tiles.append(v_i)
+            v_tiles.append(v_halves)
         offsets = held.tile([128, N // 16], U16, name="offsets")
         nc.sync.dma_start(offsets[:], offs)
 
@@ -101,36 +106,60 @@ def tile_informermodel_s_kernel(tc, q, k, v, offs, out):
 
         v_rounded_tiles = []
         for i in range(SEQS):
-            v_rounded = per_seq.tile([D, S], BF16, name="v_rounded")
-            nc.gpsimd.tensor_copy(v_rounded[:], v_tiles[i][:])
-            v_rounded_tiles.append(v_rounded)
+            v_rounded_halves = []
+            for h in range(2):
+                v_rounded = per_half.tile([D, HALF], BF16, name="v_rounded")
+                nc.gpsimd.tensor_copy(v_rounded[:], v_tiles[i][h][:])
+                v_rounded_halves.append(v_rounded)
+            v_rounded_tiles.append(v_rounded_halves)
 
-        e_tiles = [exp_of_scores(nc, per_seq, scores, q_tiles[0], k_tiles[0])]
-        v_flipped_tiles = [flip(nc, per_seq, others, v_rounded_tiles[0], identity_bf16)]
-        e_tiles.append(exp_of_scores(nc, per_seq, scores, q_tiles[1], k_tiles[1]))
-        to_place = None
-        for i in range(SEQS):
-            e, v_flipped = e_tiles[i], v_flipped_tiles[i]
-            over_den_column = reciprocal_of_den(nc, per_seq, others, e, ones)
-            if i + 1 < SEQS:
-                v_flipped_tiles.append(flip(nc, per_seq, others, v_rounded_tiles[i + 1], identity_bf16))
-            if to_place is not None:
-                place_and_store(nc, *to_place)
+        score_tiles = {}
+        e_tiles = [per_seq.tile([128, KEY_BLOCKS, N], BF16, name="e") for i in range(SEQS)]
+        v_flipped_tiles = []
+        num_sum, num, spread, window = None, None, None, None
 
-            num_sum = others.tile([D, N], F32, name="num_sum")
-            for b in range(KEY_BLOCKS):
-                nc.tensor.matmul(num_sum[:], v_flipped[:, b, :], e[:, b, :], start=(b == 0), stop=(b == KEY_BLOCKS - 1))
-            over_den = spread_over_partitions(nc, per_seq, others, over_den_column, identity)
-            num = per_seq.tile([D, N], F32, name="num")
-            nc.scalar.copy(num[:], num_sum[:])
+        def scores_of_step(g):
+            i, pair = divmod(g, PAIRS)
+            score_tiles[g] = make_scores(nc, scores, q_tiles[i], k_tiles[i], pair)
 
-            scaled_ctx = per_seq.tile([D, N], F32, name="scaled_ctx")
-            mean = per_seq.tile([D, 1], F32, name="mean")
-            nc.vector.scalar_tensor_tensor(scaled_ctx[:], num[:], 1.0 / N, over_den[:], MULT, MULT, accum_out=mean[:])
+        def exp_of_step(g):
+            i, pair = divmod(g, PAIRS)
+            first = blocks_of(pair)[0]
+            nc.scalar.activation(e_tiles[i][:, first : first + 2, :], score_tiles[g][:], EXP, scale=1.0 / math.sqrt(D))
 
-            if i + 2 < SEQS:
-                e_tiles.append(exp_of_scores(nc, per_seq, scores, q_tiles[i + 2], k_tiles[i + 2]))
-            window = per_seq.tile([D, S], F32, name="window")
-            nc.vector.tensor_scalar_add(window[:], zeros[:], mean[:])
-            to_place = (window, num, over_den, offsets, out[i * D : (i + 1) * D, :])
-        place_and_store(nc, *to_place)
+        for g in range(SCORES_AHEAD):
+            scores_of_step(g)
+        exp_of_step(0)
+        for g in range(STEPS + 1):
+            if g + SCORES_AHEAD < STEPS:
+                scores_of_step(g + SCORES_AHEAD)
+            if g + 1 < STEPS:
+                exp_of_step(g + 1)
+            if g == 0:
+                v_flipped_tiles.append(flip(nc, per_seq, others, v_rounded_tiles[0], identity_bf16))
+
+            if g > 0 and g % PAIRS == 0:
+                i = g // PAIRS - 1
+                over_den = per_seq.tile([D, N], F32, name="over_den")
+                nc.scalar.copy(over_den[:], spread[:])
+                nc.vector.tensor_tensor(window[:].indirect(offsets[:]), num[:], over_den[:], MULT)
+                nc.sync.dma_start(out[i * D : (i + 1) * D, :], window[:])
+
+            if g < STEPS:
+                i, pair = divmod(g, PAIRS)
+                if pair == 0:
+                    num_sum = others.tile([D, N], F32, name="num_sum")
+                for b in blocks_of(pair):
+                    nc.tensor.matmul(num_sum[:], v_flipped_tiles[i][:, b, :], e_tiles[i][:, b, :], start=(b == 0), stop=(b == KEY_BLOCKS - 1))
+                if pair == PAIRS - 1:
+                    over_den_column = reciprocal_of_den(nc, per_seq, others, e_tiles[i], ones)
+                    num = per_seq.tile([D, N], F32, name="num")
+                    nc.scalar.copy(num[:], num_sum[:])
+                    if i + 1 < SEQS:
+                        v_flipped_tiles.append(flip(nc, per_seq, others, v_rounded_tiles[i + 1], identity_bf16))
+                    spread = spread_over_partitions(nc, others, over_den_column, identity)
+                    scaled_ctx = per_seq.tile([D, N], F32, name="scaled_ctx")
+                    mean = per_seq.tile([D, 1], F32, name="mean")
+                    nc.vector.scalar_tensor_tensor(scaled_ctx[:], num[:], 1.0 / N, spread[:], MULT, MULT, accum_out=mean[:])
+                    window = per_seq.tile([D, S], F32, name="window")
+                    nc.vector.tensor_scalar_add(window[:], zeros[:], mean[:])

@@ -42,7 +42,7 @@ def flip(nc, per_seq, others, v_rounded_halves, identity_bf16):
         first = h * KEY_BLOCKS // 2
         for b in range(KEY_BLOCKS // 2):
             nc.tensor.transpose(flipped[:, first + b, :], v_rounded[:, b * 128 : (b + 1) * 128], identity_bf16[:])
-        nc.vector.tensor_copy(v_flipped[:, first : first + KEY_BLOCKS // 2, :], flipped[:, first : first + KEY_BLOCKS // 2, :])
+        nc.scalar.copy(v_flipped[:, first : first + KEY_BLOCKS // 2, :], flipped[:, first : first + KEY_BLOCKS // 2, :])
     return v_flipped
 
 

@@ -116,7 +116,7 @@ def tile_informermodel_s_kernel(tc, q, k, v, offs, out):
         score_tiles = {}
         e_tiles = [per_seq.tile([128, KEY_BLOCKS, N], BF16, name="e") for i in range(SEQS)]
         v_flipped_tiles = []
-        num_sum, num, spread, window = None, None, None, None
+        num_sum, num, over_den, window = None, None, None, None
 
         def scores_of_step(g):
             i, pair = divmod(g, PAIRS)
@@ -140,8 +140,6 @@ def tile_informermodel_s_kernel(tc, q, k, v, offs, out):
 
             if g > 0 and g % PAIRS == 0:
                 i = g // PAIRS - 1
-                over_den = per_seq.tile([D, N], F32, name="over_den")
-                nc.scalar.copy(over_den[:], spread[:])
                 nc.vector.tensor_tensor(window[:].indirect(offsets[:]), num[:], over_den[:], MULT)
                 nc.sync.dma_start(out[i * D : (i + 1) * D, :], window[:])
 
@@ -161,5 +159,7 @@ def tile_informermodel_s_kernel(tc, q, k, v, offs, out):
                     scaled_ctx = per_seq.tile([D, N], F32, name="scaled_ctx")
                     mean = per_seq.tile([D, 1], F32, name="mean")
                     nc.vector.scalar_tensor_tensor(scaled_ctx[:], num[:], 1.0 / N, spread[:], MULT, MULT, accum_out=mean[:])
+                    over_den = per_seq.tile([D, N], F32, name="over_den")
+                    nc.vector.tensor_copy(over_den[:], spread[:])
                     window = per_seq.tile([D, S], F32, name="window")
                     nc.vector.tensor_scalar_add(window[:], zeros[:], mean[:])

@@ -37,12 +37,14 @@ def make_scores(nc, scores, q_i, k_i, pair):
 
 def flip(nc, per_seq, others, v_rounded_halves, identity_bf16):
     flipped = others.tile([128, KEY_BLOCKS, D], BF16, name="flipped")
-    v_flipped = per_seq.tile([128, KEY_BLOCKS, D], BF16, name="v_flipped")
     for h, v_rounded in enumerate(v_rounded_halves):
         first = h * KEY_BLOCKS // 2
         for b in range(KEY_BLOCKS // 2):
             nc.tensor.transpose(flipped[:, first + b, :], v_rounded[:, b * 128 : (b + 1) * 128], identity_bf16[:])
-        nc.scalar.copy(v_flipped[:, first : first + KEY_BLOCKS // 2, :], flipped[:, first : first + KEY_BLOCKS // 2, :])
+    v_flipped = per_seq.tile([128, KEY_BLOCKS, D], BF16, name="v_flipped")
+    for h in range(2):
+        blocks = slice(h * KEY_BLOCKS // 2, (h + 1) * KEY_BLOCKS // 2)
+        nc.scalar.copy(v_flipped[:, blocks, :], flipped[:, blocks, :])
     return v_flipped
 
 

@@ -48,23 +48,20 @@ def flip(nc, per_seq, others, v_rounded_halves, identity_bf16):
     return v_flipped
 
 
-def reciprocal_of_den(nc, per_seq, others, e, ones):
-    den = others.tile([128, QUERY_BLOCKS], F32, name="den")
+def reciprocal_of_den(nc, per_seq, den, e, ones):
     for jb in range(QUERY_BLOCKS):
         queries = slice(jb * 128, (jb + 1) * 128)
         for b in range(KEY_BLOCKS):
             nc.tensor.matmul(den[:, jb : jb + 1], e[:, b, queries], ones[:], start=(b == 0), stop=(b == KEY_BLOCKS - 1))
     over_den_column = per_seq.tile([128, QUERY_BLOCKS], F32, name="over_den_column")
-    nc.vector.reciprocal(over_den_column[:], den[:])
+    nc.vector.reciprocal(over_den_column[:], den)
     return over_den_column
 
 
-def spread_over_partitions(nc, others, over_den_column, identity):
-    spread = others.tile([D, N], F32, name="spread")
+def spread_over_partitions(nc, spread, over_den_column, identity):
     for jb in range(QUERY_BLOCKS):
         repeated = over_den_column[:, jb : jb + 1].to_broadcast([128, D])
         nc.tensor.transpose(spread[:, jb * 128 : (jb + 1) * 128], repeated, identity[:])
-    return spread
 
 
 def tile_informermodel_s_kernel(tc, q, k, v, offs, out):
@@ -75,6 +72,7 @@ def tile_informermodel_s_kernel(tc, q, k, v, offs, out):
         tc.tile_pool(name="per_half", bufs=2 * SEQS) as per_half,
         tc.psum_pool(name="scores", bufs=SCORE_BANKS) as scores,
         tc.psum_pool(name="others", bufs=1) as others,
+        tc.psum_pool(name="dens", bufs=2) as dens,
     ):
         q_tiles, k_tiles, v_tiles = [], [], []
         for i in range(SEQS):
@@ -152,16 +150,18 @@ def tile_informermodel_s_kernel(tc, q, k, v, offs, out):
                 for b in blocks_of(pair):
                     nc.tensor.matmul(num_sum[:], v_flipped_tiles[i][:, b, :], e_tiles[i][:, b, :], start=(b == 0), stop=(b == KEY_BLOCKS - 1))
                 if pair == PAIRS - 1:
-                    over_den_column = reciprocal_of_den(nc, per_seq, others, e_tiles[i], ones)
+                    den_and_spread = dens.tile([128, N + QUERY_BLOCKS], F32, name="den_and_spread")
+                    spread = den_and_spread[:, 0:N]
+                    over_den_column = reciprocal_of_den(nc, per_seq, den_and_spread[:, N : N + QUERY_BLOCKS], e_tiles[i], ones)
                     num = per_seq.tile([D, N], F32, name="num")
                     nc.scalar.copy(num[:], num_sum[:])
                     if i + 1 < SEQS:
                         v_flipped_tiles.append(flip(nc, per_seq, others, v_rounded_tiles[i + 1], identity_bf16))
-                    spread = spread_over_partitions(nc, others, over_den_column, identity)
+                    spread_over_partitions(nc, spread, over_den_column, identity)
                     scaled_ctx = per_seq.tile([D, N], F32, name="scaled_ctx")
                     mean = per_seq.tile([D, 1], F32, name="mean")
-                    nc.vector.scalar_tensor_tensor(scaled_ctx[:], num[:], 1.0 / N, spread[:], MULT, MULT, accum_out=mean[:])
+                    nc.vector.scalar_tensor_tensor(scaled_ctx[:], num[:], 1.0 / N, spread, MULT, MULT, accum_out=mean[:])
                     over_den = per_seq.tile([D, N], F32, name="over_den")
-                    nc.vector.tensor_copy(over_den[:], spread[:])
+                    nc.vector.tensor_copy(over_den[:], spread)
                     window = per_seq.tile([D, S], F32, name="window")
                     nc.vector.tensor_scalar_add(window[:], zeros[:], mean[:])

@@ -51,8 +51,8 @@ def flip(nc, per_seq, others, v_rounded_halves, identity_bf16):
 def reciprocal_of_den(nc, per_seq, den, e, ones):
     for jb in range(QUERY_BLOCKS):
         queries = slice(jb * 128, (jb + 1) * 128)
-        for b in range(KEY_BLOCKS):
-            nc.tensor.matmul(den[:, jb : jb + 1], e[:, b, queries], ones[:], start=(b == 0), stop=(b == KEY_BLOCKS - 1))
+        for b in reversed(range(KEY_BLOCKS)):
+            nc.tensor.matmul(den[:, jb : jb + 1], e[:, b, queries], ones[:], start=(b == KEY_BLOCKS - 1), stop=(b == 0))
     over_den_column = per_seq.tile([128, QUERY_BLOCKS], F32, name="over_den_column")
     nc.vector.reciprocal(over_den_column[:], den)
     return over_den_column

@@ -154,14 +154,20 @@ def tile_informermodel_s_kernel(tc, q, k, v, offs, out):
                     spread = den_and_spread[:, 0:N]
                     over_den_column = reciprocal_of_den(nc, per_seq, den_and_spread[:, N : N + QUERY_BLOCKS], e_tiles[i], ones)
                     num = per_seq.tile([D, N], F32, name="num")
-                    nc.scalar.copy(num[:], num_sum[:])
+                    if i > 0:
+                        nc.scalar.copy(num[:], num_sum[:])
                     if i + 1 < SEQS:
                         v_flipped_tiles.append(flip(nc, per_seq, others, v_rounded_tiles[i + 1], identity_bf16))
                     spread_over_partitions(nc, spread, over_den_column, identity)
                     scaled_ctx = per_seq.tile([D, N], F32, name="scaled_ctx")
                     mean = per_seq.tile([D, 1], F32, name="mean")
-                    nc.vector.scalar_tensor_tensor(scaled_ctx[:], num[:], 1.0 / N, spread, MULT, MULT, accum_out=mean[:])
                     over_den = per_seq.tile([D, N], F32, name="over_den")
-                    nc.vector.tensor_copy(over_den[:], spread)
+                    if i == 0:
+                        nc.vector.tensor_copy(over_den[:], spread)
+                        nc.vector.scalar_tensor_tensor(scaled_ctx[:], num_sum[:], 1.0 / N, over_den[:], MULT, MULT, accum_out=mean[:])
+                        nc.scalar.copy(num[:], num_sum[:])
+                    else:
+                        nc.vector.scalar_tensor_tensor(scaled_ctx[:], num[:], 1.0 / N, spread, MULT, MULT, accum_out=mean[:])
+                        nc.vector.tensor_copy(over_den[:], spread)
                     window = per_seq.tile([D, S], F32, name="window")
                     nc.vector.tensor_scalar_add(window[:], zeros[:], mean[:])

@@ -150,14 +150,14 @@ def tile_informermodel_s_kernel(tc, q, k, v, offs, out):
                 for b in blocks_of(pair):
                     nc.tensor.matmul(num_sum[:], v_flipped_tiles[i][:, b, :], e_tiles[i][:, b, :], start=(b == 0), stop=(b == KEY_BLOCKS - 1))
                 if pair == PAIRS - 1:
+                    if i + 1 < SEQS:
+                        v_flipped_tiles.append(flip(nc, per_seq, others, v_rounded_tiles[i + 1], identity_bf16))
                     den_and_spread = dens.tile([128, N + QUERY_BLOCKS], F32, name="den_and_spread")
                     spread = den_and_spread[:, 0:N]
                     over_den_column = reciprocal_of_den(nc, per_seq, den_and_spread[:, N : N + QUERY_BLOCKS], e_tiles[i], ones)
                     num = per_seq.tile([D, N], F32, name="num")
                     if i > 0:
                         nc.scalar.copy(num[:], num_sum[:])
-                    if i + 1 < SEQS:
-                        v_flipped_tiles.append(flip(nc, per_seq, others, v_rounded_tiles[i + 1], identity_bf16))
                     spread_over_partitions(nc, spread, over_den_column, identity)
                     scaled_ctx = per_seq.tile([D, N], F32, name="scaled_ctx")
                     mean = per_seq.tile([D, 1], F32, name="mean")

import math

import concourse.mybir as mybir
from concourse.masks import make_identity

SEQS = 4
D = 128
S = 1024
N = 256
KEY_BLOCKS = S // 128
QUERY_BLOCKS = N // 128
HALF = S // 2
PAIRS = KEY_BLOCKS // 2
STEPS = SEQS * PAIRS
SCORE_BANKS = 4
SCORES_AHEAD = SCORE_BANKS - 1

F32 = mybir.dt.float32
BF16 = mybir.dt.bfloat16
U16 = mybir.dt.uint16
MULT = mybir.AluOpType.mult
EXP = mybir.ActivationFunctionType.Exp

FLOPS = 2 * (2 * SEQS * D * S * N)


def blocks_of(pair):
    return (2 * pair, 2 * pair + 1)


def make_scores(nc, scores, q_i, k_i, pair):
    score = scores.tile([128, 2, N], F32, name="score")
    for half, b in enumerate(blocks_of(pair)):
        nc.tensor.matmul(score[:, half, :], k_i[:, b * 128 : (b + 1) * 128], q_i[:], start=True, stop=True)
    return score


def flip(nc, per_seq, others, v_rounded_halves, identity_bf16):
    flipped = others.tile([128, KEY_BLOCKS, D], BF16, name="flipped")
    for h, v_rounded in enumerate(v_rounded_halves):
        first = h * KEY_BLOCKS // 2
        for b in range(KEY_BLOCKS // 2):
            nc.tensor.transpose(flipped[:, first + b, :], v_rounded[:, b * 128 : (b + 1) * 128], identity_bf16[:])
    v_flipped = per_seq.tile([128, KEY_BLOCKS, D], BF16, name="v_flipped")
    for h in range(2):
        blocks = slice(h * KEY_BLOCKS // 2, (h + 1) * KEY_BLOCKS // 2)
        nc.scalar.copy(v_flipped[:, blocks, :], flipped[:, blocks, :])
    return v_flipped


def reciprocal_of_den(nc, per_seq, den, e, ones):
    for jb in range(QUERY_BLOCKS):
        queries = slice(jb * 128, (jb + 1) * 128)
        for b in reversed(range(KEY_BLOCKS)):
            nc.tensor.matmul(den[:, jb : jb + 1], e[:, b, queries], ones[:], start=(b == KEY_BLOCKS - 1), stop=(b == 0))
    over_den_column = per_seq.tile([128, QUERY_BLOCKS], F32, name="over_den_column")
    nc.vector.reciprocal(over_den_column[:], den)
    return over_den_column


def spread_over_partitions(nc, spread, over_den_column, identity):
    for jb in range(QUERY_BLOCKS):
        repeated = over_den_column[:, jb : jb + 1].to_broadcast([128, D])
        nc.tensor.transpose(spread[:, jb * 128 : (jb + 1) * 128], repeated, identity[:])


def tile_informermodel_s_kernel(tc, q, k, v, offs, out):
    nc = tc.nc
    with (
        tc.tile_pool(name="held", bufs=1) as held,
        tc.tile_pool(name="per_seq", bufs=SEQS) as per_seq,
        tc.tile_pool(name="per_half", bufs=2 * SEQS) as per_half,
        tc.psum_pool(name="scores", bufs=SCORE_BANKS) as scores,
        tc.psum_pool(name="others", bufs=1) as others,
        tc.psum_pool(name="dens", bufs=2) as dens,
    ):
        q_tiles, k_tiles, v_tiles = [], [], []
        for i in range(SEQS):
            rows = slice(i * D, (i + 1) * D)
            q_i = per_seq.tile([D, N], BF16, name="q_i")
            k_i = per_seq.tile([D, S], BF16, name="k_i")
            nc.sync.dma_start(q_i[:], q[rows, :])
            pieces = PAIRS if i == 0 else 1
            for piece in range(pieces):
                columns = slice(piece * S // pieces, (piece + 1) * S // pieces)
                nc.sync.dma_start(k_i[:, columns], k[rows, columns])
            v_halves = []
            for h in range(2):
                v_half = per_half.tile([D, HALF], F32, name="v_half")
                nc.sync.dma_start(v_half[:], v[rows, h * HALF : (h + 1) * HALF])
                v_halves.append(v_half)
            q_tiles.append(q_i)
            k_tiles.append(k_i)
            v_tiles.append(v_halves)
        offsets = held.tile([128, N // 16], U16, name="offsets")
        nc.sync.dma_start(offsets[:], offs)

        identity = held.tile([128, 128], F32, name="identity")
        make_identity(nc, identity[:])
        identity_bf16 = held.tile([128, 128], BF16, name="identity_bf16")
        make_identity(nc, identity_bf16[:])
        ones = held.tile([128, 1], BF16, name="ones")
        nc.vector.memset(ones[:], 1.0)
        zeros = held.tile([D, S], F32, name="zeros")
        nc.vector.memset(zeros[:], 0.0)

        v_rounded_tiles = []
        for i in range(SEQS):
            v_rounded_halves = []
            for h in range(2):
                v_rounded = per_half.tile([D, HALF], BF16, name="v_rounded")
                nc.gpsimd.tensor_copy(v_rounded[:], v_tiles[i][h][:])
                v_rounded_halves.append(v_rounded)
            v_rounded_tiles.append(v_rounded_halves)

        score_tiles = {}
        e_tiles = [per_seq.tile([128, KEY_BLOCKS, N], BF16, name="e") for i in range(SEQS)]
        v_flipped_tiles = []
        num_sum, num, over_den, window = None, None, None, None

        def scores_of_step(g):
            i, pair = divmod(g, PAIRS)
            score_tiles[g] = make_scores(nc, scores, q_tiles[i], k_tiles[i], pair)

        def exp_of_step(g):
            i, pair = divmod(g, PAIRS)
            first = blocks_of(pair)[0]
            nc.scalar.activation(e_tiles[i][:, first : first + 2, :], score_tiles[g][:], EXP, scale=1.0 / math.sqrt(D))

        for g in range(SCORES_AHEAD):
            scores_of_step(g)
        exp_of_step(0)
        for g in range(STEPS + 1):
            if g + SCORES_AHEAD < STEPS:
                scores_of_step(g + SCORES_AHEAD)
            if g + 1 < STEPS:
                exp_of_step(g + 1)
            if g == 0:
                v_flipped_tiles.append(flip(nc, per_seq, others, v_rounded_tiles[0], identity_bf16))

            if g > 0 and g % PAIRS == 0:
                i = g // PAIRS - 1
                nc.vector.tensor_tensor(window[:].indirect(offsets[:]), num[:], over_den[:], MULT)
                nc.sync.dma_start(out[i * D : (i + 1) * D, :], window[:])

            if g < STEPS:
                i, pair = divmod(g, PAIRS)
                if pair == 0:
                    num_sum = others.tile([D, N], F32, name="num_sum")
                for b in blocks_of(pair):
                    nc.tensor.matmul(num_sum[:], v_flipped_tiles[i][:, b, :], e_tiles[i][:, b, :], start=(b == 0), stop=(b == KEY_BLOCKS - 1))
                if pair == PAIRS - 1:
                    if i + 1 < SEQS:
                        v_flipped_tiles.append(flip(nc, per_seq, others, v_rounded_tiles[i + 1], identity_bf16))
                    den_and_spread = dens.tile([128, N + QUERY_BLOCKS], F32, name="den_and_spread")
                    spread = den_and_spread[:, 0:N]
                    over_den_column = reciprocal_of_den(nc, per_seq, den_and_spread[:, N : N + QUERY_BLOCKS], e_tiles[i], ones)
                    num = per_seq.tile([D, N], F32, name="num")
                    if i > 0:
                        nc.scalar.copy(num[:], num_sum[:])
                    spread_over_partitions(nc, spread, over_den_column, identity)
                    scaled_ctx = per_seq.tile([D, N], F32, name="scaled_ctx")
                    mean = per_seq.tile([D, 1], F32, name="mean")
                    over_den = per_seq.tile([D, N], F32, name="over_den")
                    if i == 0:
                        nc.vector.tensor_copy(over_den[:], spread)
                        nc.vector.scalar_tensor_tensor(scaled_ctx[:], num_sum[:], 1.0 / N, over_den[:], MULT, MULT, accum_out=mean[:])
                        nc.scalar.copy(num[:], num_sum[:])
                    else:
                        nc.vector.scalar_tensor_tensor(scaled_ctx[:], num[:], 1.0 / N, spread, MULT, MULT, accum_out=mean[:])
                        nc.vector.tensor_copy(over_den[:], spread)
                    window = per_seq.tile([D, S], F32, name="window")
                    nc.vector.tensor_scalar_add(window[:], zeros[:], mean[:])
